import numpy as np
import ml_dtypes


def mxq(x, axis, fmt="e4m3"):
    dtype, down = {"e4m3": (ml_dtypes.float8_e4m3fn, 7), "e5m2": (ml_dtypes.float8_e5m2, 14)}[fmt]
    v = np.moveaxis(np.asarray(x, np.float32).astype(ml_dtypes.bfloat16).astype(np.float64), axis, -1)
    blocks = v.reshape(v.shape[:-1] + (-1, 32))
    amax = np.abs(blocks).max(-1, keepdims=True)
    byte = np.maximum(np.where(amax > 0, np.frexp(amax)[1] - 1 + 127, 0) - down, 1)
    scale = np.exp2(byte - 127.0)
    codes = (blocks / scale).astype(np.float32).astype(dtype).astype(np.float64)
    return np.moveaxis((codes * scale).reshape(v.shape), -1, axis)


WIDE = False


def mx_kscale(k):
    if not WIDE:
        return np.ones(k)
    levels = np.array([10, -10, 5, -5, 0])
    if k % 512:
        return np.exp2(np.random.permutation(np.resize(levels, k // 32))).repeat(32)
    a = np.empty((k // 512, 16))
    for p in range(k // 512):
        a[p, :8] = np.random.permutation(np.resize(levels, 8))
        for g in range(8):
            far = levels[np.abs(levels - a[p, g]) >= 10]
            a[p, g + 8] = far[np.random.randint(len(far))]
    return np.exp2(a.ravel()).repeat(32)


BF16 = ml_dtypes.bfloat16


def bf(x):
    return np.asarray(x, np.float32).astype(BF16)


def f64(x):
    return np.asarray(x).astype(np.float64)


E2M1 = np.array([0.0, 0.5, 1.0, 1.5, 2.0, 3.0, 4.0, 6.0, -0.0, -0.5, -1.0, -1.5, -2.0, -3.0, -4.0, -6.0])


def pack_weight(w, fmt):
    k, n = w.shape
    w = f64(bf(w)).reshape(k // 32, 32, n)
    amax = np.abs(w).max(1)
    if fmt == "e4m3":
        byte = np.frexp(amax)[1] - 1 + 127 - 7
    else:
        mant, ex = np.frexp(amax / 6.0)
        byte = np.where(mant > 0.5, ex, ex - 1) + 127
    byte = np.clip(np.where(amax > 0, byte, 1), 1, 254)
    scaled = (w * np.exp2(127.0 - byte)[:, None, :]).reshape(k, n).astype(np.float32)
    by_word = np.ascontiguousarray(scaled.reshape(k // 512, 128, 4, n).transpose(0, 1, 3, 2))
    if fmt == "e4m3":
        words = by_word.astype(ml_dtypes.float8_e4m3fn).view(np.uint8)
    else:
        c = by_word.astype(ml_dtypes.float4_e2m1fn).view(np.uint8) & 0xF
        words = c[..., 0::2] | (c[..., 1::2] << 4)
    return np.ascontiguousarray(words), np.ascontiguousarray(byte.astype(np.uint8).reshape(k // 512, 16, n))


def unpack_weight(words, scales, fmt):
    g, p, n, _ = words.shape
    if fmt == "e4m3":
        vals = np.ascontiguousarray(words).view(ml_dtypes.float8_e4m3fn).astype(np.float64)
    else:
        nib = np.empty((g, p, n, 4), np.uint8)
        nib[..., 0::2] = words & 0xF
        nib[..., 1::2] = words >> 4
        vals = E2M1[nib]
    vals = vals * np.repeat(np.exp2(scales.astype(np.float64) - 127.0), 8, axis=1)[..., None]
    return vals.transpose(0, 1, 3, 2).reshape(g * 512, n)
def pack4(w):
    words, scales = pack_weight(w, "e2m1")
    return words.reshape(words.shape[0], 128, -1), scales


def unpack4(words, scales):
    return unpack_weight(words.reshape(words.shape[0], 128, -1, 2), scales, "e2m1")


B, SIDE, HE, Z, HD, XO = 4096, 32, 1024, 512, 256, 1024


def draw0():
    n = np.random.standard_normal
    s, t = mx_kscale(HE), mx_kscale(Z)
    h = bf(np.tanh(n((B, HE))) * s)
    W_mu_e_words, W_mu_e_scales = pack4((n((Z, HE)) * 1.5 / np.sqrt(HE) / s[None, :] * t[:, None]).T)
    b_mu_e = bf(n(Z) * 0.3 * t)
    W_ls_e_words, W_ls_e_scales = pack4((n((Z, HE)) * 1.5 / np.sqrt(HE) / s[None, :]).T)
    b_ls_e = bf(n(Z) * 0.3)
    eps_z = bf(n((B, Z)) * t)
    W_in_d_words, W_in_d_scales = pack4((n((HD, Z)) * 0.6 / np.sqrt(Z) / t[None, :]).T)
    b_in_d = bf(n(HD) * 0.3)
    return {"h": h,
            "W_mu_e_words": W_mu_e_words,
            "W_mu_e_scales": W_mu_e_scales,
            "b_mu_e": b_mu_e,
            "W_ls_e_words": W_ls_e_words,
            "W_ls_e_scales": W_ls_e_scales,
            "b_ls_e": b_ls_e,
            "eps_z": eps_z,
            "W_in_d_words": W_in_d_words,
            "W_in_d_scales": W_in_d_scales,
            "b_in_d": b_in_d}


def core(h, W_mu_e_words, W_mu_e_scales, b_mu_e, W_ls_e_words, W_ls_e_scales, b_ls_e, eps_z, W_in_d_words, W_in_d_scales, b_in_d):
    hq = mxq(f64(h), 1, "e4m3")
    mu_e = (hq @ unpack4(W_mu_e_words, W_mu_e_scales)) + f64(b_mu_e)
    ls_e = (hq @ unpack4(W_ls_e_words, W_ls_e_scales)) + f64(b_ls_e)
    z = mu_e + np.exp(0.5 * ls_e) * f64(eps_z)
    return np.tanh((mxq(z, 1, "e4m3") @ unpack4(W_in_d_words, W_in_d_scales)) + f64(b_in_d))


def e4m3fn_bytes(y):
    return np.clip(np.asarray(y, np.float64), -448.0, 448.0).astype(np.float32).astype(ml_dtypes.float8_e4m3fn).view(np.uint8)


def e4m3fn_values(b):
    return np.asarray(b, np.uint8).view(ml_dtypes.float8_e4m3fn).astype(np.float64)


def setup_inputs():
    d = draw0()
    x0 = np.asarray(d['h']).astype(np.float64)
    s = (np.max(np.abs(x0), axis=(0,), keepdims=True) / 448.0).astype(np.float32)
    out = {}
    for k, v in d.items():
        if k == 'h':
            out['h_bytes'] = e4m3fn_bytes(x0 / s.astype(np.float64))
            out['h_scale'] = s
        else:
            out[k] = v
    return out


def reference(h_bytes, h_scale, W_mu_e_words, W_mu_e_scales, b_mu_e, W_ls_e_words, W_ls_e_scales, b_ls_e, eps_z, W_in_d_words, W_in_d_scales, b_in_d):
    return core(e4m3fn_values(h_bytes) * h_scale.astype(np.float64), W_mu_e_words, W_mu_e_scales, b_mu_e, W_ls_e_words, W_ls_e_scales, b_ls_e, eps_z, W_in_d_words, W_in_d_scales, b_in_d)

@@ -1,0 +1,363 @@
+from contextlib import ExitStack
+
+import concourse.mybir as mybir
+from concourse.masks import make_identity
+
+B, HE, Z, HD = 4096, 1024, 512, 256
+FLOPS = 2 * B * HE * 2 * Z + 2 * B * Z * HD
+
+F32 = mybir.dt.float32
+BF16 = mybir.dt.bfloat16
+I32 = mybir.dt.int32
+U32 = mybir.dt.uint32
+U8 = mybir.dt.uint8
+E4M3 = mybir.dt.float8_e4m3fn
+E4M3X4 = mybir.dt.float8_e4m3fn_x4
+E2M1X4 = mybir.dt.float4_e2m1fn_x4
+ADD = mybir.AluOpType.add
+MULT = mybir.AluOpType.mult
+ACT = mybir.ActivationFunctionType
+
+P = 128
+T = 512
+J = T // P
+NB = B // T
+G = HE // 512
+
+
+def tile_vae_pa_t_w4_kernel(
+    tc,
+    h_bytes,
+    h_scale,
+    W_mu_e_words,
+    W_mu_e_scales,
+    b_mu_e,
+    W_ls_e_words,
+    W_ls_e_scales,
+    b_ls_e,
+    eps_z,
+    W_in_d_words,
+    W_in_d_scales,
+    b_in_d,
+    out,
+):
+    nc = tc.nc
+    h_blocks = h_bytes.rearrange("(b p j) k -> b p (j k)", p=P, j=J)
+    eps_blocks = eps_z.rearrange("(b p j) n -> b p (j n)", p=P, j=J)
+    out_blocks = out.rearrange("(b p j) n -> b p (j n)", p=P, j=J)
+
+    with ExitStack() as ctx:
+        const = ctx.enter_context(tc.tile_pool(name="const", bufs=1))
+        loads = ctx.enter_context(tc.tile_pool(name="loads", bufs=NB))
+        work = ctx.enter_context(tc.tile_pool(name="work", bufs=2))
+        ps_tr = ctx.enter_context(tc.psum_pool(name="ps_tr", bufs=2))
+        ps_eps = ctx.enter_context(tc.psum_pool(name="ps_eps", bufs=2))
+        ps_sx = ctx.enter_context(tc.psum_pool(name="ps_sx", bufs=2))
+        ps_mu = ctx.enter_context(tc.psum_pool(name="ps_mu", bufs=2))
+
+        w_raw = const.tile([P, 2, G, 1024], U8, align_bytes=64)
+        w_perm = const.tile([P, 2, G, 1024], U8, align_bytes=64)
+        s_raw = const.tile([P, 2, G, 512], U8, align_bytes=64)
+        s_perm = const.tile([P, 2, G, 512], U8, align_bytes=64)
+        wd = const.tile([P, 512], U8, align_bytes=64)
+        sd = const.tile([P, 256], U8, align_bytes=64)
+        scale = const.tile([P, 2, HE], F32)
+        ident = const.tile([P, P], F32)
+        b_mu = const.tile([P, 4], BF16)
+        b_ls = const.tile([P, 4], BF16)
+        b_ls_half = const.tile([P, 4], F32)
+        b_out = const.tile([P, 2, 2], BF16)
+        warm = const.tile([P, 1], F32)
+
+        h_tiles = []
+        eps_tiles = []
+        for b in range(NB):
+            h_in = loads.tile([P, J * HE], U8, align_bytes=64)
+            h_tiles.append(h_in)
+            eps_in = loads.tile([P, J * Z], BF16, align_bytes=64)
+            eps_tiles.append(eps_in)
+
+        with tc.manual_schedule():
+            nc.vector.memset(s_raw[:].rearrange("p w g n -> p (w g n)").bitcast(I32), 0)
+            nc.vector.memset(sd[:].bitcast(I32), 0)
+            nc.vector.memset(warm[:], 0.0)
+            nc.scalar.activation(out=warm[:], in_=warm[:], func=ACT.Exp)
+            make_identity(nc, ident[:])
+
+            nc.scalar.dma_start(out=scale[:, 0, :], in_=h_scale.rearrange("o k -> (o k)").partition_broadcast(P))
+            nc.sync.dma_start(out=w_raw[:, 0, :, :], in_=W_mu_e_words.rearrange("g p n -> p g n"))
+            nc.sync.dma_start(out=w_raw[:, 1, :, :], in_=W_ls_e_words.rearrange("g p n -> p g n"))
+            for c in range(2):
+                half = slice(c * 2 * HE, (c + 1) * 2 * HE)
+                nc.sync.dma_start(out=h_tiles[0][:, half], in_=h_blocks[0][:, half])
+            for w, src in ((0, W_mu_e_scales), (1, W_ls_e_scales)):
+                rows = src.rearrange("g (q r) n -> r q g n", r=4)
+                for r in range(4):
+                    nc.sync.dma_start(out=s_raw[r : P : 32, w, :, :].bitcast(I32), in_=rows[r].bitcast(I32))
+            nc.sync.dma_start(out=eps_tiles[0][:], in_=eps_blocks[0])
+            nc.sync.dma_start(out=b_ls[:], in_=b_ls_e.rearrange("(p t) -> p t", t=4))
+            nc.sync.dma_start(out=b_mu[:], in_=b_mu_e.rearrange("(p t) -> p t", t=4))
+            nc.sync.dma_start(out=h_tiles[1][:], in_=h_blocks[1])
+            nc.sync.dma_start(out=wd[:], in_=W_in_d_words[0])
+            rows_d = W_in_d_scales[0].rearrange("(q r) n -> r q n", r=4)
+            for r in range(4):
+                nc.sync.dma_start(out=sd[r : P : 32, :].bitcast(I32), in_=rows_d[r].bitcast(I32))
+            nc.sync.dma_start(out=b_out[:, :, 0], in_=b_in_d.rearrange("(c p) -> p c", p=P))
+            nc.sync.dma_start(out=eps_tiles[1][:], in_=eps_blocks[1])
+            for b in range(2, NB):
+                nc.sync.dma_start(out=h_tiles[b][:], in_=h_blocks[b])
+                nc.sync.dma_start(out=eps_tiles[b][:], in_=eps_blocks[b])
+
+            nc.scalar.copy(out=scale[:, 1, :], in_=scale[:, 0, :])
+
+            for w in range(2):
+                for g in range(G):
+                    nc.vector.tensor_copy(
+                        out=w_perm[:, w, g, :].rearrange("p (t m e) -> p t m e", t=4, e=2),
+                        in_=w_raw[:, w, g, :].rearrange("p (m t e) -> p t m e", t=4, e=2),
+                    )
+
+            st = {}
+
+            def v_product(b, half):
+                if half == 0:
+                    hb = work.tile([P, J * HE], BF16, align_bytes=64, name="hb")
+                    st["hb", b] = hb
+                hb = st["hb", b]
+                width = HE if b == 0 else 2 * HE
+                for c in range(half * 2 * HE, (half + 1) * 2 * HE, width):
+                    nc.vector.tensor_tensor(
+                        out=hb[:, c : c + width],
+                        in0=h_tiles[b][:, c : c + width].bitcast(E4M3),
+                        in1=scale[:].rearrange("p a k -> p (a k)")[:, :width],
+                        op=MULT,
+                    )
+
+            def h_turn(b, jp, g):
+                words = st["hb", b][:].bitcast(F32)
+                bank = ps_tr.tile([P, 2, 256], F32, name="bank_tr")
+                for jj in range(2):
+                    for u in range(2):
+                        first = (2 * jp + jj) * 512 + 256 * g + u
+                        nc.tensor.transpose(bank[:, u, jj * P : (jj + 1) * P], words[:, first : first + 255 : 2], ident[:])
+                if jp == 0 and g == 0:
+                    hg = work.tile([P, G, T * 4], BF16, align_bytes=64, name="hg")
+                    st["hg", b] = hg
+                st["bank", b, jp, g] = bank
+
+            def h_out(b, jp, g):
+                words = st["hg", b][:, g, jp * 1024 : (jp + 1) * 1024].bitcast(F32)
+                nc.scalar.copy(
+                    out=words.rearrange("p (r u) -> p r u", u=2),
+                    in_=st["bank", b, jp, g][:].rearrange("p u r -> p r u"),
+                )
+
+            def v_quant_h(b):
+                hq = work.tile([P, G, T], U32, align_bytes=64, name="hq")
+                hs = work.tile([P, G, T], U8, align_bytes=64, name="hs")
+                st["hq", b] = (hq, hs)
+                nc.vector.quantize_mx(
+                    out=hq[:].rearrange("p g n -> p (g n)").bitcast(E4M3X4),
+                    scales=hs[:].rearrange("p g n -> p (g n)"),
+                    in_=st["hg", b][:].rearrange("p g n -> p (g n)"),
+                )
+
+            def first_matmul(acc, b, w, t):
+                hq, hs = st["hq", b]
+                for g in range(G):
+                    nc.tensor.matmul_mx(
+                        out=acc[:],
+                        lhsT=w_perm[:, w, g, t * 256 : (t + 1) * 256].bitcast(E2M1X4),
+                        lhsT_scale=s_perm[:, w, g, t * P : (t + 1) * P],
+                        rhs=hq[:, g, :].bitcast(E4M3X4),
+                        rhs_scale=hs[:, g, :],
+                        start=(g == 0),
+                        stop=(g == G - 1),
+                    )
+
+            def mm_mu(b, t):
+                acc = ps_mu.tile([P, T], F32, name="acc_mu")
+                st["mu", b, t] = acc
+                first_matmul(acc, b, 0, t)
+
+            def mm_ls(b, t):
+                acc = ps_sx.tile([P, T], F32, name="acc_sx")
+                st["ls", b, t] = acc
+                first_matmul(acc, b, 1, t)
+
+            def s_exp(b, t):
+                if t == 0:
+                    e = work.tile([P, 4, T], F32, name="e")
+                    st["e", b] = e
+                nc.scalar.activation(
+                    out=st["e", b][:, t, :], in_=st["ls", b, t][:], func=ACT.Exp, bias=b_ls_half[:, t : t + 1], scale=0.5
+                )
+
+            def eps_turn(b, u):
+                words = eps_tiles[b][:].bitcast(F32)
+                bank = ps_eps.tile([P, T], F32, name="bank_eps")
+                st["eps", b, u] = bank
+                for j in range(J):
+                    first = j * 256 + u
+                    nc.tensor.transpose(bank[:, j * P : (j + 1) * P], words[:, first : first + 255 : 2], ident[:])
+
+            def v_noise(b, u):
+                if u == 0:
+                    noise = work.tile([P, 4, T], F32, name="noise")
+                    st["noise", b] = noise
+                nc.vector.tensor_tensor(
+                    out=st["noise", b][:, 2 * u : 2 * u + 2, :],
+                    in0=st["eps", b, u][:].bitcast(BF16).rearrange("p (r e) -> p e r", e=2),
+                    in1=st["e", b][:, 2 * u : 2 * u + 2, :],
+                    op=MULT,
+                )
+
+            def v_z(b, t):
+                if t == 0:
+                    zt = work.tile([P, 4, T], BF16, align_bytes=64, name="zt")
+                    st["zt", b] = zt
+                nc.vector.scalar_tensor_tensor(
+                    out=st["zt", b][:, t, :],
+                    in0=st["mu", b, t][:],
+                    scalar=b_mu[:, t : t + 1],
+                    in1=st["noise", b][:, t, :],
+                    op0=ADD,
+                    op1=ADD,
+                )
+
+            def z_interleave(engine, b, half):
+                if half == 0:
+                    zg = work.tile([P, T, 4], BF16, align_bytes=64, name="zg")
+                    st["zg", b] = zg
+                cols = slice(half * 256, (half + 1) * 256)
+                src = st["zt", b][:, :, cols].rearrange("p t r -> p r t")
+                dst = st["zg", b][:, cols, :]
+                if engine == "scalar":
+                    nc.scalar.copy(out=dst, in_=src)
+                else:
+                    nc.vector.tensor_copy(out=dst, in_=src)
+
+            def v_quant_z(b):
+                zq = work.tile([P, T], U32, align_bytes=64, name="zq")
+                zs = work.tile([P, T], U8, align_bytes=64, name="zs")
+                st["zq", b] = (zq, zs)
+                nc.vector.quantize_mx(
+                    out=zq[:].bitcast(E4M3X4), scales=zs[:], in_=st["zg", b][:].rearrange("p r t -> p (r t)")
+                )
+
+            def mm_out(b, c):
+                zq, zs = st["zq", b]
+                acc = ps_sx.tile([P, T], F32, name="acc_sx")
+                st["o", b, c] = acc
+                nc.tensor.matmul_mx(
+                    out=acc[:],
+                    lhsT=wd[:, c * 256 : (c + 1) * 256].bitcast(E2M1X4),
+                    lhsT_scale=sd[:, c * P : (c + 1) * P],
+                    rhs=zq[:].bitcast(E4M3X4),
+                    rhs_scale=zs[:],
+                    start=True,
+                    stop=True,
+                )
+
+            def s_tanh(b, c):
+                if c == 0:
+                    o = work.tile([P, 2, T], F32, name="o")
+                    st["ot", b] = o
+                nc.scalar.activation(
+                    out=st["ot", b][:, c, :], in_=st["o", b, c][:], func=ACT.Tanh, bias=b_out[:, c, 0:1], scale=1.0
+                )
+
+            def out_turn(b, jp):
+                bank = ps_tr.tile([P, 2, 256], F32, name="bank_tr")
+                st["obank", b, jp] = bank
+                for jj in range(2):
+                    for c in range(2):
+                        j = 2 * jp + jj
+                        nc.tensor.transpose(
+                            bank[:, jj, c * P : (c + 1) * P], st["ot", b][:, c, j * P : (j + 1) * P], ident[:]
+                        )
+
+            def out_copy(b, jp):
+                if jp == 0:
+                    y = work.tile([P, J, HD], F32, name="y")
+                    st["y", b] = y
+                nc.scalar.copy(out=st["y", b][:, 2 * jp : 2 * jp + 2, :], in_=st["obank", b, jp][:])
+
+            def store(b):
+                nc.sync.dma_start(out=out_blocks[b], in_=st["y", b][:].rearrange("p j n -> p (j n)"))
+
+            for s in range(-2, NB + 1):
+                now = 0 <= s < NB
+                nxt = 0 <= s + 1 < NB
+                far = 0 <= s + 2 < NB
+                old = 0 <= s - 1 < NB
+                if now:
+                    mm_mu(s, 0)
+                    mm_mu(s, 1)
+                    v_noise(s, 0)
+                if old:
+                    z_interleave("scalar", s - 1, 0)
+                if nxt:
+                    for g in range(G):
+                        h_turn(s + 1, 0, g)
+                    for g in range(G):
+                        h_out(s + 1, 0, g)
+                if far:
+                    v_product(s + 2, 0)
+                if s == -2:
+                    nc.vector.tensor_scalar(out=b_ls_half[:], in0=b_ls[:], scalar1=0.5, scalar2=None, op0=MULT)
+                    nc.vector.tensor_copy(
+                        out=s_perm[:].rearrange("p w g (t m) -> p (w g) t m", t=4),
+                        in_=s_raw[:].rearrange("p w g (m t) -> p (w g) t m", t=4),
+                    )
+                if now:
+                    mm_ls(s, 2)
+                    mm_ls(s, 3)
+                if old:
+                    z_interleave("vector" if s == NB else "scalar", s - 1, 1)
+                if now:
+                    s_exp(s, 2)
+                    s_exp(s, 3)
+                    v_z(s, 0)
+                    v_z(s, 1)
+                if nxt:
+                    for g in range(G):
+                        h_turn(s + 1, 1, g)
+                    for g in range(G):
+                        h_out(s + 1, 1, g)
+                if old:
+                    v_quant_z(s - 1)
+                if nxt:
+                    eps_turn(s + 1, 0)
+                if now:
+                    mm_mu(s, 2)
+                    mm_mu(s, 3)
+                if old:
+                    mm_out(s - 1, 0)
+                    mm_out(s - 1, 1)
+                if now:
+                    v_noise(s, 1)
+                if old:
+                    s_tanh(s - 1, 0)
+                    s_tanh(s - 1, 1)
+                if nxt:
+                    v_quant_h(s + 1)
+                if old:
+                    out_turn(s - 1, 0)
+                    out_turn(s - 1, 1)
+                if nxt:
+                    eps_turn(s + 1, 1)
+                if far:
+                    v_product(s + 2, 1)
+                if nxt:
+                    mm_ls(s + 1, 0)
+                    mm_ls(s + 1, 1)
+                    s_exp(s + 1, 0)
+                    s_exp(s + 1, 1)
+                if old:
+                    out_copy(s - 1, 0)
+                    out_copy(s - 1, 1)
+                    store(s - 1)
+                if now:
+                    v_z(s, 2)
+                    v_z(s, 3)

@@ -50,8 +50,8 @@ def tile_vae_pa_t_w4_kernel(
         const = ctx.enter_context(tc.tile_pool(name="const", bufs=1))
         loads = ctx.enter_context(tc.tile_pool(name="loads", bufs=NB))
         work = ctx.enter_context(tc.tile_pool(name="work", bufs=2))
+        ps_h = ctx.enter_context(tc.psum_pool(name="ps_h", bufs=2))
         ps_tr = ctx.enter_context(tc.psum_pool(name="ps_tr", bufs=2))
-        ps_eps = ctx.enter_context(tc.psum_pool(name="ps_eps", bufs=2))
         ps_sx = ctx.enter_context(tc.psum_pool(name="ps_sx", bufs=2))
         ps_mu = ctx.enter_context(tc.psum_pool(name="ps_mu", bufs=2))
 
@@ -61,7 +61,7 @@ def tile_vae_pa_t_w4_kernel(
         s_perm = const.tile([P, 2, G, 512], U8, align_bytes=64)
         wd = const.tile([P, 512], U8, align_bytes=64)
         sd = const.tile([P, 256], U8, align_bytes=64)
-        scale = const.tile([P, 2, HE], F32)
+        scale = const.tile([P, G, 4], F32)
         ident = const.tile([P, P], F32)
         b_mu = const.tile([P, 4], BF16)
         b_ls = const.tile([P, 4], BF16)
@@ -77,19 +77,19 @@ def tile_vae_pa_t_w4_kernel(
             eps_in = loads.tile([P, J * Z], BF16, align_bytes=64)
             eps_tiles.append(eps_in)
 
-        with tc.manual_schedule():
+        with tc.manual_schedule(engines={mybir.EngineType.SP}):
             nc.vector.memset(s_raw[:].rearrange("p w g n -> p (w g n)").bitcast(I32), 0)
             nc.vector.memset(sd[:].bitcast(I32), 0)
             nc.vector.memset(warm[:], 0.0)
             nc.scalar.activation(out=warm[:], in_=warm[:], func=ACT.Exp)
             make_identity(nc, ident[:])
 
-            nc.scalar.dma_start(out=scale[:, 0, :], in_=h_scale.rearrange("o k -> (o k)").partition_broadcast(P))
-            nc.sync.dma_start(out=w_raw[:, 0, :, :], in_=W_mu_e_words.rearrange("g p n -> p g n"))
-            nc.sync.dma_start(out=w_raw[:, 1, :, :], in_=W_ls_e_words.rearrange("g p n -> p g n"))
             for c in range(2):
                 half = slice(c * 2 * HE, (c + 1) * 2 * HE)
                 nc.sync.dma_start(out=h_tiles[0][:, half], in_=h_blocks[0][:, half])
+            nc.sync.dma_start(out=scale[:], in_=h_scale.rearrange("o (g p t) -> p (o g) t", p=P, t=4))
+            nc.sync.dma_start(out=w_raw[:, 0, :, :], in_=W_mu_e_words.rearrange("g p n -> p g n"))
+            nc.sync.dma_start(out=w_raw[:, 1, :, :], in_=W_ls_e_words.rearrange("g p n -> p g n"))
             for w, src in ((0, W_mu_e_scales), (1, W_ls_e_scales)):
                 rows = src.rearrange("g (q r) n -> r q g n", r=4)
                 for r in range(4):
@@ -108,8 +108,6 @@ def tile_vae_pa_t_w4_kernel(
                 nc.sync.dma_start(out=h_tiles[b][:], in_=h_blocks[b])
                 nc.sync.dma_start(out=eps_tiles[b][:], in_=eps_blocks[b])
 
-            nc.scalar.copy(out=scale[:, 1, :], in_=scale[:, 0, :])
-
             for w in range(2):
                 for g in range(G):
                     nc.vector.tensor_copy(
@@ -119,23 +117,16 @@ def tile_vae_pa_t_w4_kernel(
 
             st = {}
 
-            def v_product(b, half):
-                if half == 0:
+            def s_widen(b, q):
+                if q == 0:
                     hb = work.tile([P, J * HE], BF16, align_bytes=64, name="hb")
                     st["hb", b] = hb
-                hb = st["hb", b]
-                width = HE if b == 0 else 2 * HE
-                for c in range(half * 2 * HE, (half + 1) * 2 * HE, width):
-                    nc.vector.tensor_tensor(
-                        out=hb[:, c : c + width],
-                        in0=h_tiles[b][:, c : c + width].bitcast(E4M3),
-                        in1=scale[:].rearrange("p a k -> p (a k)")[:, :width],
-                        op=MULT,
-                    )
+                cols = slice(q * HE, (q + 1) * HE)
+                nc.scalar.copy(out=st["hb", b][:, cols], in_=h_tiles[b][:, cols].bitcast(E4M3))
 
             def h_turn(b, jp, g):
                 words = st["hb", b][:].bitcast(F32)
-                bank = ps_tr.tile([P, 2, 256], F32, name="bank_tr")
+                bank = ps_h.tile([P, 2, 256], F32, name="bank_h")
                 for jj in range(2):
                     for u in range(2):
                         first = (2 * jp + jj) * 512 + 256 * g + u
@@ -145,11 +136,12 @@ def tile_vae_pa_t_w4_kernel(
                     st["hg", b] = hg
                 st["bank", b, jp, g] = bank
 
-            def h_out(b, jp, g):
-                words = st["hg", b][:, g, jp * 1024 : (jp + 1) * 1024].bitcast(F32)
-                nc.scalar.copy(
-                    out=words.rearrange("p (r u) -> p r u", u=2),
-                    in_=st["bank", b, jp, g][:].rearrange("p u r -> p r u"),
+            def v_scale(b, jp, g):
+                nc.vector.tensor_tensor(
+                    out=st["hg", b][:, g, jp * 1024 : (jp + 1) * 1024].rearrange("p (r u e) -> p r u e", u=2, e=2),
+                    in0=st["bank", b, jp, g][:].bitcast(BF16).rearrange("p u (r e) -> p r u e", e=2),
+                    in1=scale[:, g, :].unsqueeze(1).to_broadcast([P, 256, 4]).rearrange("p r (u e) -> p r u e", u=2),
+                    op=MULT,
                 )
 
             def v_quant_h(b):
@@ -195,20 +187,26 @@ def tile_vae_pa_t_w4_kernel(
 
             def eps_turn(b, u):
                 words = eps_tiles[b][:].bitcast(F32)
-                bank = ps_eps.tile([P, T], F32, name="bank_eps")
+                bank = ps_tr.tile([P, 2, 256], F32, name="bank_tr")
                 st["eps", b, u] = bank
                 for j in range(J):
                     first = j * 256 + u
-                    nc.tensor.transpose(bank[:, j * P : (j + 1) * P], words[:, first : first + 255 : 2], ident[:])
+                    nc.tensor.transpose(bank[:, j // 2, (j % 2) * P : (j % 2 + 1) * P], words[:, first : first + 255 : 2], ident[:])
 
-            def v_noise(b, u):
+            def s_eps(b, u):
                 if u == 0:
+                    epsT = work.tile([P, 2, T], F32, name="epsT")
+                    st["epsT", b] = epsT
+                nc.scalar.copy(out=st["epsT", b][:, u, :], in_=st["eps", b, u][:].rearrange("p a r -> p (a r)"))
+
+            def noise_mul(engine, b, t):
+                if t == 0:
                     noise = work.tile([P, 4, T], F32, name="noise")
                     st["noise", b] = noise
-                nc.vector.tensor_tensor(
-                    out=st["noise", b][:, 2 * u : 2 * u + 2, :],
-                    in0=st["eps", b, u][:].bitcast(BF16).rearrange("p (r e) -> p e r", e=2),
-                    in1=st["e", b][:, 2 * u : 2 * u + 2, :],
+                engine.tensor_tensor(
+                    out=st["noise", b][:, t, :],
+                    in0=st["epsT", b][:, t // 2, :].bitcast(BF16).rearrange("p (r e) -> p e r", e=2)[:, t % 2, :],
+                    in1=st["e", b][:, t, :],
                     op=MULT,
                 )
 
@@ -232,8 +230,8 @@ def tile_vae_pa_t_w4_kernel(
                 cols = slice(half * 256, (half + 1) * 256)
                 src = st["zt", b][:, :, cols].rearrange("p t r -> p r t")
                 dst = st["zg", b][:, cols, :]
-                if engine == "scalar":
-                    nc.scalar.copy(out=dst, in_=src)
+                if engine == "gpsimd":
+                    nc.gpsimd.tensor_scalar(out=dst, in0=src, scalar1=1.0, scalar2=0.0, op0=MULT, op1=ADD)
                 else:
                     nc.vector.tensor_copy(out=dst, in_=src)
 
@@ -286,24 +284,36 @@ def tile_vae_pa_t_w4_kernel(
             def store(b):
                 nc.sync.dma_start(out=out_blocks[b], in_=st["y", b][:].rearrange("p j n -> p (j n)"))
 
-            for s in range(-2, NB + 1):
+            for s in range(-2, NB + 2):
                 now = 0 <= s < NB
                 nxt = 0 <= s + 1 < NB
                 far = 0 <= s + 2 < NB
                 old = 0 <= s - 1 < NB
-                if now:
-                    mm_mu(s, 0)
-                    mm_mu(s, 1)
-                    v_noise(s, 0)
-                if old:
-                    z_interleave("scalar", s - 1, 0)
-                if nxt:
-                    for g in range(G):
-                        h_turn(s + 1, 0, g)
-                    for g in range(G):
-                        h_out(s + 1, 0, g)
+                end = 0 <= s - 2 < NB
+                last = s >= NB
                 if far:
-                    v_product(s + 2, 0)
+                    s_widen(s + 2, 0)
+                if now:
+                    mm_ls(s, 0)
+                    mm_ls(s, 1)
+                    s_exp(s, 0)
+                    s_exp(s, 1)
+                    noise_mul(nc.gpsimd, s, 0)
+                    noise_mul(nc.gpsimd, s, 1)
+                if far:
+                    s_widen(s + 2, 1)
+                if nxt:
+                    h_turn(s + 1, 0, 0)
+                    v_scale(s + 1, 0, 0)
+                if old:
+                    v_z(s - 1, 2)
+                if nxt:
+                    h_turn(s + 1, 0, 1)
+                    v_scale(s + 1, 0, 1)
+                if old:
+                    v_z(s - 1, 3)
+                    z_interleave("gpsimd", s - 1, 0)
+                    z_interleave("vector" if last else "gpsimd", s - 1, 1)
                 if s == -2:
                     nc.vector.tensor_scalar(out=b_ls_half[:], in0=b_ls[:], scalar1=0.5, scalar2=None, op0=MULT)
                     nc.vector.tensor_copy(
@@ -313,51 +323,46 @@ def tile_vae_pa_t_w4_kernel(
                 if now:
                     mm_ls(s, 2)
                     mm_ls(s, 3)
-                if old:
-                    z_interleave("vector" if s == NB else "scalar", s - 1, 1)
-                if now:
                     s_exp(s, 2)
                     s_exp(s, 3)
-                    v_z(s, 0)
-                    v_z(s, 1)
-                if nxt:
-                    for g in range(G):
-                        h_turn(s + 1, 1, g)
-                    for g in range(G):
-                        h_out(s + 1, 1, g)
-                if old:
-                    v_quant_z(s - 1)
+                    noise_mul(nc.gpsimd, s, 2)
+                    noise_mul(nc.gpsimd, s, 3)
                 if nxt:
                     eps_turn(s + 1, 0)
+                    s_eps(s + 1, 0)
+                if far:
+                    s_widen(s + 2, 2)
+                if nxt:
+                    h_turn(s + 1, 1, 0)
+                    v_scale(s + 1, 1, 0)
                 if now:
-                    mm_mu(s, 2)
-                    mm_mu(s, 3)
+                    mm_mu(s, 0)
+                    v_z(s, 0)
+                if nxt:
+                    h_turn(s + 1, 1, 1)
+                    v_scale(s + 1, 1, 1)
+                    eps_turn(s + 1, 1)
+                    s_eps(s + 1, 1)
                 if old:
+                    v_quant_z(s - 1)
                     mm_out(s - 1, 0)
                     mm_out(s - 1, 1)
                 if now:
-                    v_noise(s, 1)
+                    mm_mu(s, 1)
+                    v_z(s, 1)
                 if old:
                     s_tanh(s - 1, 0)
                     s_tanh(s - 1, 1)
+                if far:
+                    s_widen(s + 2, 3)
                 if nxt:
                     v_quant_h(s + 1)
                 if old:
                     out_turn(s - 1, 0)
                     out_turn(s - 1, 1)
-                if nxt:
-                    eps_turn(s + 1, 1)
-                if far:
-                    v_product(s + 2, 1)
-                if nxt:
-                    mm_ls(s + 1, 0)
-                    mm_ls(s + 1, 1)
-                    s_exp(s + 1, 0)
-                    s_exp(s + 1, 1)
-                if old:
                     out_copy(s - 1, 0)
                     out_copy(s - 1, 1)
                     store(s - 1)
                 if now:
-                    v_z(s, 2)
-                    v_z(s, 3)
+                    mm_mu(s, 2)
+                    mm_mu(s, 3)

@@ -19,6 +19,7 @@ MULT = mybir.AluOpType.mult
 ACT = mybir.ActivationFunctionType
 
 P = 128
+NLAST = 1
 T = 512
 J = T // P
 NB = B // T
@@ -51,7 +52,7 @@ def tile_vae_pa_t_w4_kernel(
         loads = ctx.enter_context(tc.tile_pool(name="loads", bufs=NB))
         work = ctx.enter_context(tc.tile_pool(name="work", bufs=2))
         ps_h = ctx.enter_context(tc.psum_pool(name="ps_h", bufs=2))
-        ps_tr = ctx.enter_context(tc.psum_pool(name="ps_tr", bufs=2))
+        ps_e = ctx.enter_context(tc.psum_pool(name="ps_e", bufs=2))
         ps_sx = ctx.enter_context(tc.psum_pool(name="ps_sx", bufs=2))
         ps_mu = ctx.enter_context(tc.psum_pool(name="ps_mu", bufs=2))
 
@@ -77,7 +78,7 @@ def tile_vae_pa_t_w4_kernel(
             eps_in = loads.tile([P, J * Z], BF16, align_bytes=64)
             eps_tiles.append(eps_in)
 
-        with tc.manual_schedule(engines={mybir.EngineType.SP}):
+        with tc.manual_schedule():
             nc.vector.memset(s_raw[:].rearrange("p w g n -> p (w g n)").bitcast(I32), 0)
             nc.vector.memset(sd[:].bitcast(I32), 0)
             nc.vector.memset(warm[:], 0.0)
@@ -94,9 +95,9 @@ def tile_vae_pa_t_w4_kernel(
                 rows = src.rearrange("g (q r) n -> r q g n", r=4)
                 for r in range(4):
                     nc.sync.dma_start(out=s_raw[r : P : 32, w, :, :].bitcast(I32), in_=rows[r].bitcast(I32))
-            nc.sync.dma_start(out=eps_tiles[0][:], in_=eps_blocks[0])
             nc.sync.dma_start(out=b_ls[:], in_=b_ls_e.rearrange("(p t) -> p t", t=4))
             nc.sync.dma_start(out=b_mu[:], in_=b_mu_e.rearrange("(p t) -> p t", t=4))
+            nc.sync.dma_start(out=eps_tiles[0][:], in_=eps_blocks[0])
             nc.sync.dma_start(out=h_tiles[1][:], in_=h_blocks[1])
             nc.sync.dma_start(out=wd[:], in_=W_in_d_words[0])
             rows_d = W_in_d_scales[0].rearrange("(q r) n -> r q n", r=4)
@@ -117,9 +118,12 @@ def tile_vae_pa_t_w4_kernel(
 
             st = {}
 
+            def first(key):
+                return key not in st
+
             def s_widen(b, q):
-                if q == 0:
-                    hb = work.tile([P, J * HE], BF16, align_bytes=64, name="hb")
+                if first(("hb", b)):
+                    hb = work.tile([P, J * HE], BF16, align_bytes=64, name="hb", bufs=3)
                     st["hb", b] = hb
                 cols = slice(q * HE, (q + 1) * HE)
                 nc.scalar.copy(out=st["hb", b][:, cols], in_=h_tiles[b][:, cols].bitcast(E4M3))
@@ -129,9 +133,9 @@ def tile_vae_pa_t_w4_kernel(
                 bank = ps_h.tile([P, 2, 256], F32, name="bank_h")
                 for jj in range(2):
                     for u in range(2):
-                        first = (2 * jp + jj) * 512 + 256 * g + u
-                        nc.tensor.transpose(bank[:, u, jj * P : (jj + 1) * P], words[:, first : first + 255 : 2], ident[:])
-                if jp == 0 and g == 0:
+                        w0 = (2 * jp + jj) * 512 + 256 * g + u
+                        nc.tensor.transpose(bank[:, u, jj * P : (jj + 1) * P], words[:, w0 : w0 + 255 : 2], ident[:])
+                if first(("hg", b)):
                     hg = work.tile([P, G, T * 4], BF16, align_bytes=64, name="hg")
                     st["hg", b] = hg
                 st["bank", b, jp, g] = bank
@@ -145,6 +149,12 @@ def tile_vae_pa_t_w4_kernel(
                 )
 
             def v_quant_h(b):
+                if b == 0:
+                    nc.vector.tensor_copy(
+                        out=s_perm[:].rearrange("p w g (t m) -> p (w g) t m", t=4),
+                        in_=s_raw[:].rearrange("p w g (m t) -> p (w g) t m", t=4),
+                    )
+                    nc.vector.tensor_scalar(out=b_ls_half[:], in0=b_ls[:], scalar1=0.5, scalar2=None, op0=MULT)
                 hq = work.tile([P, G, T], U32, align_bytes=64, name="hq")
                 hs = work.tile([P, G, T], U8, align_bytes=64, name="hs")
                 st["hq", b] = (hq, hs)
@@ -178,7 +188,7 @@ def tile_vae_pa_t_w4_kernel(
                 first_matmul(acc, b, 1, t)
 
             def s_exp(b, t):
-                if t == 0:
+                if first(("e", b)):
                     e = work.tile([P, 4, T], F32, name="e")
                     st["e", b] = e
                 nc.scalar.activation(
@@ -187,53 +197,43 @@ def tile_vae_pa_t_w4_kernel(
 
             def eps_turn(b, u):
                 words = eps_tiles[b][:].bitcast(F32)
-                bank = ps_tr.tile([P, 2, 256], F32, name="bank_tr")
+                bank = ps_e.tile([P, T], F32, name="bank_e")
                 st["eps", b, u] = bank
                 for j in range(J):
-                    first = j * 256 + u
-                    nc.tensor.transpose(bank[:, j // 2, (j % 2) * P : (j % 2 + 1) * P], words[:, first : first + 255 : 2], ident[:])
+                    w0 = j * 256 + u
+                    nc.tensor.transpose(bank[:, j * P : (j + 1) * P], words[:, w0 : w0 + 255 : 2], ident[:])
 
-            def s_eps(b, u):
-                if u == 0:
-                    epsT = work.tile([P, 2, T], F32, name="epsT")
-                    st["epsT", b] = epsT
-                nc.scalar.copy(out=st["epsT", b][:, u, :], in_=st["eps", b, u][:].rearrange("p a r -> p (a r)"))
-
-            def noise_mul(engine, b, t):
-                if t == 0:
+            def v_noise(b, u):
+                if first(("noise", b)):
                     noise = work.tile([P, 4, T], F32, name="noise")
                     st["noise", b] = noise
-                engine.tensor_tensor(
-                    out=st["noise", b][:, t, :],
-                    in0=st["epsT", b][:, t // 2, :].bitcast(BF16).rearrange("p (r e) -> p e r", e=2)[:, t % 2, :],
-                    in1=st["e", b][:, t, :],
+                nc.vector.tensor_tensor(
+                    out=st["noise", b][:, 2 * u : 2 * u + 2, :],
+                    in0=st["eps", b, u][:].bitcast(BF16).rearrange("p (r e) -> p e r", e=2),
+                    in1=st["e", b][:, 2 * u : 2 * u + 2, :],
                     op=MULT,
                 )
 
-            def v_z(b, t):
-                if t == 0:
-                    zt = work.tile([P, 4, T], BF16, align_bytes=64, name="zt")
-                    st["zt", b] = zt
-                nc.vector.scalar_tensor_tensor(
-                    out=st["zt", b][:, t, :],
-                    in0=st["mu", b, t][:],
-                    scalar=b_mu[:, t : t + 1],
-                    in1=st["noise", b][:, t, :],
-                    op0=ADD,
-                    op1=ADD,
+            def s_mu(b, t):
+                if first(("mu_b", b)):
+                    mu_b = work.tile([P, 4, T], F32, name="mu_b")
+                    st["mu_b", b] = mu_b
+                nc.scalar.activation(
+                    out=st["mu_b", b][:, t, :], in_=st["mu", b, t][:], func=ACT.Identity, bias=b_mu[:, t : t + 1], scale=1.0
                 )
 
-            def z_interleave(engine, b, half):
-                if half == 0:
+            def z_sum(b, half):
+                if first(("zg", b)):
                     zg = work.tile([P, T, 4], BF16, align_bytes=64, name="zg")
                     st["zg", b] = zg
                 cols = slice(half * 256, (half + 1) * 256)
-                src = st["zt", b][:, :, cols].rearrange("p t r -> p r t")
-                dst = st["zg", b][:, cols, :]
-                if engine == "gpsimd":
-                    nc.gpsimd.tensor_scalar(out=dst, in0=src, scalar1=1.0, scalar2=0.0, op0=MULT, op1=ADD)
-                else:
-                    nc.vector.tensor_copy(out=dst, in_=src)
+                engine = nc.vector if b >= NB - NLAST else nc.gpsimd
+                engine.tensor_tensor(
+                    out=st["zg", b][:, cols, :],
+                    in0=st["mu_b", b][:, :, cols].rearrange("p t r -> p r t"),
+                    in1=st["noise", b][:, :, cols].rearrange("p t r -> p r t"),
+                    op=ADD,
+                )
 
             def v_quant_z(b):
                 zq = work.tile([P, T], U32, align_bytes=64, name="zq")
@@ -258,7 +258,7 @@ def tile_vae_pa_t_w4_kernel(
                 )
 
             def s_tanh(b, c):
-                if c == 0:
+                if first(("ot", b)):
                     o = work.tile([P, 2, T], F32, name="o")
                     st["ot", b] = o
                 nc.scalar.activation(
@@ -266,7 +266,7 @@ def tile_vae_pa_t_w4_kernel(
                 )
 
             def out_turn(b, jp):
-                bank = ps_tr.tile([P, 2, 256], F32, name="bank_tr")
+                bank = ps_e.tile([P, 2, 256], F32, name="bank_e")
                 st["obank", b, jp] = bank
                 for jj in range(2):
                     for c in range(2):
@@ -276,93 +276,41 @@ def tile_vae_pa_t_w4_kernel(
                         )
 
             def out_copy(b, jp):
-                if jp == 0:
-                    y = work.tile([P, J, HD], F32, name="y")
+                if first(("y", b)):
+                    y = work.tile([P, J, HD], F32, name="y", bufs=4)
                     st["y", b] = y
-                nc.scalar.copy(out=st["y", b][:, 2 * jp : 2 * jp + 2, :], in_=st["obank", b, jp][:])
+                copy = nc.scalar.copy if jp == 0 else nc.vector.tensor_copy
+                copy(out=st["y", b][:, 2 * jp : 2 * jp + 2, :], in_=st["obank", b, jp][:])
 
             def store(b):
                 nc.sync.dma_start(out=out_blocks[b], in_=st["y", b][:].rearrange("p j n -> p (j n)"))
 
-            for s in range(-2, NB + 2):
-                now = 0 <= s < NB
-                nxt = 0 <= s + 1 < NB
-                far = 0 <= s + 2 < NB
-                old = 0 <= s - 1 < NB
-                end = 0 <= s - 2 < NB
-                last = s >= NB
-                if far:
-                    s_widen(s + 2, 0)
-                if now:
-                    mm_ls(s, 0)
-                    mm_ls(s, 1)
-                    s_exp(s, 0)
-                    s_exp(s, 1)
-                    noise_mul(nc.gpsimd, s, 0)
-                    noise_mul(nc.gpsimd, s, 1)
-                if far:
-                    s_widen(s + 2, 1)
-                if nxt:
-                    h_turn(s + 1, 0, 0)
-                    v_scale(s + 1, 0, 0)
-                if old:
-                    v_z(s - 1, 2)
-                if nxt:
-                    h_turn(s + 1, 0, 1)
-                    v_scale(s + 1, 0, 1)
-                if old:
-                    v_z(s - 1, 3)
-                    z_interleave("gpsimd", s - 1, 0)
-                    z_interleave("vector" if last else "gpsimd", s - 1, 1)
-                if s == -2:
-                    nc.vector.tensor_scalar(out=b_ls_half[:], in0=b_ls[:], scalar1=0.5, scalar2=None, op0=MULT)
-                    nc.vector.tensor_copy(
-                        out=s_perm[:].rearrange("p w g (t m) -> p (w g) t m", t=4),
-                        in_=s_raw[:].rearrange("p w g (m t) -> p (w g) t m", t=4),
-                    )
-                if now:
-                    mm_ls(s, 2)
-                    mm_ls(s, 3)
-                    s_exp(s, 2)
-                    s_exp(s, 3)
-                    noise_mul(nc.gpsimd, s, 2)
-                    noise_mul(nc.gpsimd, s, 3)
-                if nxt:
-                    eps_turn(s + 1, 0)
-                    s_eps(s + 1, 0)
-                if far:
-                    s_widen(s + 2, 2)
-                if nxt:
-                    h_turn(s + 1, 1, 0)
-                    v_scale(s + 1, 1, 0)
-                if now:
-                    mm_mu(s, 0)
-                    v_z(s, 0)
-                if nxt:
-                    h_turn(s + 1, 1, 1)
-                    v_scale(s + 1, 1, 1)
-                    eps_turn(s + 1, 1)
-                    s_eps(s + 1, 1)
-                if old:
-                    v_quant_z(s - 1)
-                    mm_out(s - 1, 0)
-                    mm_out(s - 1, 1)
-                if now:
-                    mm_mu(s, 1)
-                    v_z(s, 1)
-                if old:
-                    s_tanh(s - 1, 0)
-                    s_tanh(s - 1, 1)
-                if far:
-                    s_widen(s + 2, 3)
-                if nxt:
-                    v_quant_h(s + 1)
-                if old:
-                    out_turn(s - 1, 0)
-                    out_turn(s - 1, 1)
-                    out_copy(s - 1, 0)
-                    out_copy(s - 1, 1)
-                    store(s - 1)
-                if now:
-                    mm_mu(s, 2)
-                    mm_mu(s, 3)
+            ops = {
+                "X0": lambda b: s_widen(b, 0), "X1": lambda b: s_widen(b, 1), "X2": lambda b: s_widen(b, 2), "X3": lambda b: s_widen(b, 3),
+                "T00": lambda b: h_turn(b, 0, 0), "T01": lambda b: h_turn(b, 0, 1), "T10": lambda b: h_turn(b, 1, 0), "T11": lambda b: h_turn(b, 1, 1),
+                "E00": lambda b: v_scale(b, 0, 0), "E01": lambda b: v_scale(b, 0, 1), "E10": lambda b: v_scale(b, 1, 0), "E11": lambda b: v_scale(b, 1, 1),
+                "QH": v_quant_h, "QZ": v_quant_z, "ST": store,
+                "Te0": lambda b: eps_turn(b, 0), "Te1": lambda b: eps_turn(b, 1),
+                "A0": lambda b: v_noise(b, 0), "A2": lambda b: v_noise(b, 1),
+                "I0": lambda b: z_sum(b, 0), "I1": lambda b: z_sum(b, 1),
+                "Mo0": lambda b: mm_out(b, 0), "Mo1": lambda b: mm_out(b, 1), "Y0": lambda b: s_tanh(b, 0), "Y1": lambda b: s_tanh(b, 1),
+                "To0": lambda b: out_turn(b, 0), "To1": lambda b: out_turn(b, 1), "Z0": lambda b: out_copy(b, 0), "Z1": lambda b: out_copy(b, 1),
+                "Ml0": lambda b: mm_ls(b, 0), "Ml1": lambda b: mm_ls(b, 1), "Ml2": lambda b: mm_ls(b, 2), "Ml3": lambda b: mm_ls(b, 3),
+                "Mm0": lambda b: mm_mu(b, 0), "Mm1": lambda b: mm_mu(b, 1), "Mm2": lambda b: mm_mu(b, 2), "Mm3": lambda b: mm_mu(b, 3),
+                "X_0": lambda b: s_exp(b, 0), "X_1": lambda b: s_exp(b, 1), "X_2": lambda b: s_exp(b, 2), "X_3": lambda b: s_exp(b, 3),
+                "D0": lambda b: s_mu(b, 0), "D1": lambda b: s_mu(b, 1), "D2": lambda b: s_mu(b, 2), "D3": lambda b: s_mu(b, 3),
+            }
+            order = [
+                ("Te1", 1), ("E10", -1), ("X0", -2), ("T11", -1), ("A0", 1), ("ST", 7),
+                ("T00", -1), ("QH", 0), ("D3", 1), ("Ml2", 1), ("X_2", 1), ("Ml3", 1),
+                ("X_3", 1), ("Mm0", 1), ("To1", 6), ("Mm1", 1), ("E11", -1), ("Ml1", 0),
+                ("E00", -1), ("D0", 1), ("Mm2", 1), ("A2", 1), ("D1", 1), ("Z1", 6),
+                ("Ml0", 0), ("QZ", 3), ("X_1", 0), ("D2", 1), ("T01", -1), ("T10", -2),
+                ("X_0", 0), ("To0", 6), ("X1", -3), ("Te0", 0), ("X2", -3), ("I0", 2),
+                ("Mo1", 4), ("Mo0", 4), ("Z0", 6), ("Y1", 4), ("E01", -1), ("I1", 1),
+                ("Y0", 4), ("X3", -4), ("Mm3", 0),
+            ]
+            for s in range(min(lag for name, lag in order), NB + max(lag for name, lag in order)):
+                for name, lag in order:
+                    if 0 <= s - lag < NB:
+                        ops[name](s - lag)

@@ -85,36 +85,33 @@ def tile_vae_pa_t_w4_kernel(
             nc.scalar.activation(out=warm[:], in_=warm[:], func=ACT.Exp)
             make_identity(nc, ident[:])
 
-            for c in range(2):
-                half = slice(c * 2 * HE, (c + 1) * 2 * HE)
-                nc.sync.dma_start(out=h_tiles[0][:, half], in_=h_blocks[0][:, half])
+            for q in range(J):
+                cols = slice(q * HE, (q + 1) * HE)
+                nc.sync.dma_start(out=h_tiles[0][:, cols], in_=h_blocks[0][:, cols])
             nc.sync.dma_start(out=scale[:], in_=h_scale.rearrange("o (g p t) -> p (o g) t", p=P, t=4))
-            nc.sync.dma_start(out=w_raw[:, 0, :, :], in_=W_mu_e_words.rearrange("g p n -> p g n"))
             nc.sync.dma_start(out=w_raw[:, 1, :, :], in_=W_ls_e_words.rearrange("g p n -> p g n"))
-            for w, src in ((0, W_mu_e_scales), (1, W_ls_e_scales)):
+            nc.sync.dma_start(out=w_raw[:, 0, :, :], in_=W_mu_e_words.rearrange("g p n -> p g n"))
+            nc.sync.dma_start(out=h_tiles[1][:], in_=h_blocks[1])
+            for w, src in ((1, W_ls_e_scales), (0, W_mu_e_scales)):
                 rows = src.rearrange("g (q r) n -> r q g n", r=4)
                 for r in range(4):
                     nc.sync.dma_start(out=s_raw[r : P : 32, w, :, :].bitcast(I32), in_=rows[r].bitcast(I32))
             nc.sync.dma_start(out=b_ls[:], in_=b_ls_e.rearrange("(p t) -> p t", t=4))
             nc.sync.dma_start(out=b_mu[:], in_=b_mu_e.rearrange("(p t) -> p t", t=4))
             nc.sync.dma_start(out=eps_tiles[0][:], in_=eps_blocks[0])
-            nc.sync.dma_start(out=h_tiles[1][:], in_=h_blocks[1])
+            nc.sync.dma_start(out=h_tiles[2][:], in_=h_blocks[2])
+            nc.sync.dma_start(out=eps_tiles[1][:], in_=eps_blocks[1])
+            nc.sync.dma_start(out=h_tiles[3][:], in_=h_blocks[3])
             nc.sync.dma_start(out=wd[:], in_=W_in_d_words[0])
             rows_d = W_in_d_scales[0].rearrange("(q r) n -> r q n", r=4)
             for r in range(4):
                 nc.sync.dma_start(out=sd[r : P : 32, :].bitcast(I32), in_=rows_d[r].bitcast(I32))
             nc.sync.dma_start(out=b_out[:, :, 0], in_=b_in_d.rearrange("(c p) -> p c", p=P))
-            nc.sync.dma_start(out=eps_tiles[1][:], in_=eps_blocks[1])
-            for b in range(2, NB):
+            nc.sync.dma_start(out=eps_tiles[2][:], in_=eps_blocks[2])
+            for b in range(4, NB):
                 nc.sync.dma_start(out=h_tiles[b][:], in_=h_blocks[b])
-                nc.sync.dma_start(out=eps_tiles[b][:], in_=eps_blocks[b])
-
-            for w in range(2):
-                for g in range(G):
-                    nc.vector.tensor_copy(
-                        out=w_perm[:, w, g, :].rearrange("p (t m e) -> p t m e", t=4, e=2),
-                        in_=w_raw[:, w, g, :].rearrange("p (m t e) -> p t m e", t=4, e=2),
-                    )
+                nc.sync.dma_start(out=eps_tiles[b - 1][:], in_=eps_blocks[b - 1])
+            nc.sync.dma_start(out=eps_tiles[NB - 1][:], in_=eps_blocks[NB - 1])
 
             st = {}
 
@@ -126,7 +123,10 @@ def tile_vae_pa_t_w4_kernel(
                     hb = work.tile([P, J * HE], BF16, align_bytes=64, name="hb", bufs=3)
                     st["hb", b] = hb
                 cols = slice(q * HE, (q + 1) * HE)
-                nc.scalar.copy(out=st["hb", b][:, cols], in_=h_tiles[b][:, cols].bitcast(E4M3))
+                copy = nc.vector.tensor_copy if b == 0 and q % 2 else nc.scalar.copy
+                copy(out=st["hb", b][:, cols], in_=h_tiles[b][:, cols].bitcast(E4M3))
+                if b == 0 and q == 3:
+                    permute_words(1)
 
             def h_turn(b, jp, g):
                 words = st["hb", b][:].bitcast(F32)
@@ -148,12 +148,22 @@ def tile_vae_pa_t_w4_kernel(
                     op=MULT,
                 )
 
+            def permute_words(w):
+                for g in range(G):
+                    nc.vector.tensor_copy(
+                        out=w_perm[:, w, g, :].rearrange("p (t m e) -> p t m e", t=4, e=2),
+                        in_=w_raw[:, w, g, :].rearrange("p (m t e) -> p t m e", t=4, e=2),
+                    )
+
+            def permute_scales(w):
+                nc.vector.tensor_copy(
+                    out=s_perm[:, w, :, :].rearrange("p g (t m) -> p g t m", t=4),
+                    in_=s_raw[:, w, :, :].rearrange("p g (m t) -> p g t m", t=4),
+                )
+
             def v_quant_h(b):
                 if b == 0:
-                    nc.vector.tensor_copy(
-                        out=s_perm[:].rearrange("p w g (t m) -> p (w g) t m", t=4),
-                        in_=s_raw[:].rearrange("p w g (m t) -> p (w g) t m", t=4),
-                    )
+                    permute_scales(1)
                     nc.vector.tensor_scalar(out=b_ls_half[:], in0=b_ls[:], scalar1=0.5, scalar2=None, op0=MULT)
                 hq = work.tile([P, G, T], U32, align_bytes=64, name="hq")
                 hs = work.tile([P, G, T], U8, align_bytes=64, name="hs")
@@ -163,6 +173,9 @@ def tile_vae_pa_t_w4_kernel(
                     scales=hs[:].rearrange("p g n -> p (g n)"),
                     in_=st["hg", b][:].rearrange("p g n -> p (g n)"),
                 )
+                if b == 0:
+                    permute_words(0)
+                    permute_scales(0)
 
             def first_matmul(acc, b, w, t):
                 hq, hs = st["hq", b]
@@ -229,9 +242,9 @@ def tile_vae_pa_t_w4_kernel(
                 cols = slice(half * 256, (half + 1) * 256)
                 engine = nc.vector if b >= NB - NLAST else nc.gpsimd
                 engine.tensor_tensor(
-                    out=st["zg", b][:, cols, :],
-                    in0=st["mu_b", b][:, :, cols].rearrange("p t r -> p r t"),
-                    in1=st["noise", b][:, :, cols].rearrange("p t r -> p r t"),
+                    out=st["zg", b][:, cols, :].rearrange("p (c i) t -> p c t i", i=4),
+                    in0=st["mu_b", b][:, :, cols].rearrange("p t (c i) -> p c t i", i=4),
+                    in1=st["noise", b][:, :, cols].rearrange("p t (c i) -> p c t i", i=4),
                     op=ADD,
                 )
 
@@ -301,14 +314,14 @@ def tile_vae_pa_t_w4_kernel(
                 "D0": lambda b: s_mu(b, 0), "D1": lambda b: s_mu(b, 1), "D2": lambda b: s_mu(b, 2), "D3": lambda b: s_mu(b, 3),
             }
             order = [
-                ("Te1", 1), ("E10", -1), ("X0", -2), ("T11", -1), ("A0", 1), ("ST", 7),
-                ("T00", -1), ("QH", 0), ("D3", 1), ("Ml2", 1), ("X_2", 1), ("Ml3", 1),
-                ("X_3", 1), ("Mm0", 1), ("To1", 6), ("Mm1", 1), ("E11", -1), ("Ml1", 0),
-                ("E00", -1), ("D0", 1), ("Mm2", 1), ("A2", 1), ("D1", 1), ("Z1", 6),
-                ("Ml0", 0), ("QZ", 3), ("X_1", 0), ("D2", 1), ("T01", -1), ("T10", -2),
-                ("X_0", 0), ("To0", 6), ("X1", -3), ("Te0", 0), ("X2", -3), ("I0", 2),
-                ("Mo1", 4), ("Mo0", 4), ("Z0", 6), ("Y1", 4), ("E01", -1), ("I1", 1),
-                ("Y0", 4), ("X3", -4), ("Mm3", 0),
+                ("I0", 3), ("T11", -1), ("QZ", 4), ("Mm3", 1), ("Ml3", 1), ("QH", 0),
+                ("Ml2", 0), ("Z0", 7), ("D3", 1), ("Mm0", 1), ("E10", -1), ("A0", 1),
+                ("X_3", 1), ("Te1", 1), ("T01", -1), ("X2", -3), ("X_2", 0), ("Mo1", 5),
+                ("Ml0", 0), ("D0", 1), ("E11", -1), ("X1", -3), ("Mm1", 1), ("Y1", 5),
+                ("X_0", 0), ("I1", 2), ("D1", 1), ("Mo0", 5), ("Y0", 5), ("A2", 1),
+                ("E01", -1), ("To1", 6), ("X0", -3), ("T00", -1), ("Z1", 6), ("Ml1", 0),
+                ("Mm2", 1), ("E00", -1), ("X3", -4), ("To0", 6), ("Te0", 0), ("T10", -2),
+                ("X_1", 0), ("D2", 1), ("ST", 7),
             ]
             for s in range(min(lag for name, lag in order), NB + max(lag for name, lag in order)):
                 for name, lag in order:

from contextlib import ExitStack

import concourse.mybir as mybir
from concourse.masks import make_identity

B, HE, Z, HD = 4096, 1024, 512, 256
FLOPS = 2 * B * HE * 2 * Z + 2 * B * Z * HD

F32 = mybir.dt.float32
BF16 = mybir.dt.bfloat16
I32 = mybir.dt.int32
U32 = mybir.dt.uint32
U8 = mybir.dt.uint8
E4M3 = mybir.dt.float8_e4m3fn
E4M3X4 = mybir.dt.float8_e4m3fn_x4
E2M1X4 = mybir.dt.float4_e2m1fn_x4
ADD = mybir.AluOpType.add
MULT = mybir.AluOpType.mult
ACT = mybir.ActivationFunctionType

P = 128
NLAST = 1
T = 512
J = T // P
NB = B // T
G = HE // 512


def tile_vae_pa_t_w4_kernel(
    tc,
    h_bytes,
    h_scale,
    W_mu_e_words,
    W_mu_e_scales,
    b_mu_e,
    W_ls_e_words,
    W_ls_e_scales,
    b_ls_e,
    eps_z,
    W_in_d_words,
    W_in_d_scales,
    b_in_d,
    out,
):
    nc = tc.nc
    h_blocks = h_bytes.rearrange("(b p j) k -> b p (j k)", p=P, j=J)
    eps_blocks = eps_z.rearrange("(b p j) n -> b p (j n)", p=P, j=J)
    out_blocks = out.rearrange("(b p j) n -> b p (j n)", p=P, j=J)

    with ExitStack() as ctx:
        const = ctx.enter_context(tc.tile_pool(name="const", bufs=1))
        loads = ctx.enter_context(tc.tile_pool(name="loads", bufs=NB))
        work = ctx.enter_context(tc.tile_pool(name="work", bufs=2))
        ps_h = ctx.enter_context(tc.psum_pool(name="ps_h", bufs=2))
        ps_e = ctx.enter_context(tc.psum_pool(name="ps_e", bufs=2))
        ps_sx = ctx.enter_context(tc.psum_pool(name="ps_sx", bufs=2))
        ps_mu = ctx.enter_context(tc.psum_pool(name="ps_mu", bufs=2))

        w_raw = const.tile([P, 2, G, 1024], U8, align_bytes=64)
        w_perm = const.tile([P, 2, G, 1024], U8, align_bytes=64)
        s_raw = const.tile([P, 2, G, 512], U8, align_bytes=64)
        s_perm = const.tile([P, 2, G, 512], U8, align_bytes=64)
        wd = const.tile([P, 512], U8, align_bytes=64)
        sd = const.tile([P, 256], U8, align_bytes=64)
        scale = const.tile([P, G, 4], F32)
        ident = const.tile([P, P], F32)
        b_mu = const.tile([P, 4], BF16)
        b_ls = const.tile([P, 4], BF16)
        b_ls_half = const.tile([P, 4], F32)
        b_out = const.tile([P, 2, 2], BF16)
        warm = const.tile([P, 1], F32)

        h_tiles = []
        eps_tiles = []
        for b in range(NB):
            h_in = loads.tile([P, J * HE], U8, align_bytes=64)
            h_tiles.append(h_in)
            eps_in = loads.tile([P, J * Z], BF16, align_bytes=64)
            eps_tiles.append(eps_in)

        with tc.manual_schedule():
            nc.vector.memset(s_raw[:].rearrange("p w g n -> p (w g n)").bitcast(I32), 0)
            nc.vector.memset(sd[:].bitcast(I32), 0)
            nc.vector.memset(warm[:], 0.0)
            nc.scalar.activation(out=warm[:], in_=warm[:], func=ACT.Exp)
            make_identity(nc, ident[:])

            for q in range(J):
                cols = slice(q * HE, (q + 1) * HE)
                nc.sync.dma_start(out=h_tiles[0][:, cols], in_=h_blocks[0][:, cols])
            nc.sync.dma_start(out=scale[:], in_=h_scale.rearrange("o (g p t) -> p (o g) t", p=P, t=4))
            nc.sync.dma_start(out=w_raw[:, 1, :, :], in_=W_ls_e_words.rearrange("g p n -> p g n"))
            nc.sync.dma_start(out=w_raw[:, 0, :, :], in_=W_mu_e_words.rearrange("g p n -> p g n"))
            nc.sync.dma_start(out=h_tiles[1][:], in_=h_blocks[1])
            for w, src in ((1, W_ls_e_scales), (0, W_mu_e_scales)):
                rows = src.rearrange("g (q r) n -> r q g n", r=4)
                for r in range(4):
                    nc.sync.dma_start(out=s_raw[r : P : 32, w, :, :].bitcast(I32), in_=rows[r].bitcast(I32))
            nc.sync.dma_start(out=b_ls[:], in_=b_ls_e.rearrange("(p t) -> p t", t=4))
            nc.sync.dma_start(out=b_mu[:], in_=b_mu_e.rearrange("(p t) -> p t", t=4))
            nc.sync.dma_start(out=eps_tiles[0][:], in_=eps_blocks[0])
            nc.sync.dma_start(out=h_tiles[2][:], in_=h_blocks[2])
            nc.sync.dma_start(out=eps_tiles[1][:], in_=eps_blocks[1])
            nc.sync.dma_start(out=h_tiles[3][:], in_=h_blocks[3])
            nc.sync.dma_start(out=wd[:], in_=W_in_d_words[0])
            rows_d = W_in_d_scales[0].rearrange("(q r) n -> r q n", r=4)
            for r in range(4):
                nc.sync.dma_start(out=sd[r : P : 32, :].bitcast(I32), in_=rows_d[r].bitcast(I32))
            nc.sync.dma_start(out=b_out[:, :, 0], in_=b_in_d.rearrange("(c p) -> p c", p=P))
            nc.sync.dma_start(out=eps_tiles[2][:], in_=eps_blocks[2])
            for b in range(4, NB):
                nc.sync.dma_start(out=h_tiles[b][:], in_=h_blocks[b])
                nc.sync.dma_start(out=eps_tiles[b - 1][:], in_=eps_blocks[b - 1])
            nc.sync.dma_start(out=eps_tiles[NB - 1][:], in_=eps_blocks[NB - 1])

            st = {}

            def first(key):
                return key not in st

            def s_widen(b, q):
                if first(("hb", b)):
                    hb = work.tile([P, J * HE], BF16, align_bytes=64, name="hb", bufs=3)
                    st["hb", b] = hb
                cols = slice(q * HE, (q + 1) * HE)
                copy = nc.vector.tensor_copy if b == 0 and q % 2 else nc.scalar.copy
                copy(out=st["hb", b][:, cols], in_=h_tiles[b][:, cols].bitcast(E4M3))
                if b == 0 and q == 3:
                    permute_words(1)

            def h_turn(b, jp, g):
                words = st["hb", b][:].bitcast(F32)
                bank = ps_h.tile([P, 2, 256], F32, name="bank_h")
                for jj in range(2):
                    for u in range(2):
                        w0 = (2 * jp + jj) * 512 + 256 * g + u
                        nc.tensor.transpose(bank[:, u, jj * P : (jj + 1) * P], words[:, w0 : w0 + 255 : 2], ident[:])
                if first(("hg", b)):
                    hg = work.tile([P, G, T * 4], BF16, align_bytes=64, name="hg")
                    st["hg", b] = hg
                st["bank", b, jp, g] = bank

            def v_scale(b, jp, g):
                nc.vector.tensor_tensor(
                    out=st["hg", b][:, g, jp * 1024 : (jp + 1) * 1024].rearrange("p (r u e) -> p r u e", u=2, e=2),
                    in0=st["bank", b, jp, g][:].bitcast(BF16).rearrange("p u (r e) -> p r u e", e=2),
                    in1=scale[:, g, :].unsqueeze(1).to_broadcast([P, 256, 4]).rearrange("p r (u e) -> p r u e", u=2),
                    op=MULT,
                )

            def permute_words(w):
                for g in range(G):
                    nc.vector.tensor_copy(
                        out=w_perm[:, w, g, :].rearrange("p (t m e) -> p t m e", t=4, e=2),
                        in_=w_raw[:, w, g, :].rearrange("p (m t e) -> p t m e", t=4, e=2),
                    )

            def permute_scales(w):
                nc.vector.tensor_copy(
                    out=s_perm[:, w, :, :].rearrange("p g (t m) -> p g t m", t=4),
                    in_=s_raw[:, w, :, :].rearrange("p g (m t) -> p g t m", t=4),
                )

            def v_quant_h(b):
                if b == 0:
                    permute_scales(1)
                    nc.vector.tensor_scalar(out=b_ls_half[:], in0=b_ls[:], scalar1=0.5, scalar2=None, op0=MULT)
                hq = work.tile([P, G, T], U32, align_bytes=64, name="hq")
                hs = work.tile([P, G, T], U8, align_bytes=64, name="hs")
                st["hq", b] = (hq, hs)
                nc.vector.quantize_mx(
                    out=hq[:].rearrange("p g n -> p (g n)").bitcast(E4M3X4),
                    scales=hs[:].rearrange("p g n -> p (g n)"),
                    in_=st["hg", b][:].rearrange("p g n -> p (g n)"),
                )
                if b == 0:
                    permute_words(0)
                    permute_scales(0)

            def first_matmul(acc, b, w, t):
                hq, hs = st["hq", b]
                for g in range(G):
                    nc.tensor.matmul_mx(
                        out=acc[:],
                        lhsT=w_perm[:, w, g, t * 256 : (t + 1) * 256].bitcast(E2M1X4),
                        lhsT_scale=s_perm[:, w, g, t * P : (t + 1) * P],
                        rhs=hq[:, g, :].bitcast(E4M3X4),
                        rhs_scale=hs[:, g, :],
                        start=(g == 0),
                        stop=(g == G - 1),
                    )

            def mm_mu(b, t):
                acc = ps_mu.tile([P, T], F32, name="acc_mu")
                st["mu", b, t] = acc
                first_matmul(acc, b, 0, t)

            def mm_ls(b, t):
                acc = ps_sx.tile([P, T], F32, name="acc_sx")
                st["ls", b, t] = acc
                first_matmul(acc, b, 1, t)

            def s_exp(b, t):
                if first(("e", b)):
                    e = work.tile([P, 4, T], F32, name="e")
                    st["e", b] = e
                nc.scalar.activation(
                    out=st["e", b][:, t, :], in_=st["ls", b, t][:], func=ACT.Exp, bias=b_ls_half[:, t : t + 1], scale=0.5
                )

            def eps_turn(b, u):
                words = eps_tiles[b][:].bitcast(F32)
                bank = ps_e.tile([P, T], F32, name="bank_e")
                st["eps", b, u] = bank
                for j in range(J):
                    w0 = j * 256 + u
                    nc.tensor.transpose(bank[:, j * P : (j + 1) * P], words[:, w0 : w0 + 255 : 2], ident[:])

            def v_noise(b, u):
                if first(("noise", b)):
                    noise = work.tile([P, 4, T], F32, name="noise")
                    st["noise", b] = noise
                nc.vector.tensor_tensor(
                    out=st["noise", b][:, 2 * u : 2 * u + 2, :],
                    in0=st["eps", b, u][:].bitcast(BF16).rearrange("p (r e) -> p e r", e=2),
                    in1=st["e", b][:, 2 * u : 2 * u + 2, :],
                    op=MULT,
                )

            def s_mu(b, t):
                if first(("mu_b", b)):
                    mu_b = work.tile([P, 4, T], F32, name="mu_b")
                    st["mu_b", b] = mu_b
                nc.scalar.activation(
                    out=st["mu_b", b][:, t, :], in_=st["mu", b, t][:], func=ACT.Identity, bias=b_mu[:, t : t + 1], scale=1.0
                )

            def z_sum(b, half):
                if first(("zg", b)):
                    zg = work.tile([P, T, 4], BF16, align_bytes=64, name="zg")
                    st["zg", b] = zg
                cols = slice(half * 256, (half + 1) * 256)
                engine = nc.vector if b >= NB - NLAST else nc.gpsimd
                engine.tensor_tensor(
                    out=st["zg", b][:, cols, :].rearrange("p (c i) t -> p c t i", i=4),
                    in0=st["mu_b", b][:, :, cols].rearrange("p t (c i) -> p c t i", i=4),
                    in1=st["noise", b][:, :, cols].rearrange("p t (c i) -> p c t i", i=4),
                    op=ADD,
                )

            def v_quant_z(b):
                zq = work.tile([P, T], U32, align_bytes=64, name="zq")
                zs = work.tile([P, T], U8, align_bytes=64, name="zs")
                st["zq", b] = (zq, zs)
                nc.vector.quantize_mx(
                    out=zq[:].bitcast(E4M3X4), scales=zs[:], in_=st["zg", b][:].rearrange("p r t -> p (r t)")
                )

            def mm_out(b, c):
                zq, zs = st["zq", b]
                acc = ps_sx.tile([P, T], F32, name="acc_sx")
                st["o", b, c] = acc
                nc.tensor.matmul_mx(
                    out=acc[:],
                    lhsT=wd[:, c * 256 : (c + 1) * 256].bitcast(E2M1X4),
                    lhsT_scale=sd[:, c * P : (c + 1) * P],
                    rhs=zq[:].bitcast(E4M3X4),
                    rhs_scale=zs[:],
                    start=True,
                    stop=True,
                )

            def s_tanh(b, c):
                if first(("ot", b)):
                    o = work.tile([P, 2, T], F32, name="o")
                    st["ot", b] = o
                nc.scalar.activation(
                    out=st["ot", b][:, c, :], in_=st["o", b, c][:], func=ACT.Tanh, bias=b_out[:, c, 0:1], scale=1.0
                )

            def out_turn(b, jp):
                bank = ps_e.tile([P, 2, 256], F32, name="bank_e")
                st["obank", b, jp] = bank
                for jj in range(2):
                    for c in range(2):
                        j = 2 * jp + jj
                        nc.tensor.transpose(
                            bank[:, jj, c * P : (c + 1) * P], st["ot", b][:, c, j * P : (j + 1) * P], ident[:]
                        )

            def out_copy(b, jp):
                if first(("y", b)):
                    y = work.tile([P, J, HD], F32, name="y", bufs=4)
                    st["y", b] = y
                copy = nc.scalar.copy if jp == 0 else nc.vector.tensor_copy
                copy(out=st["y", b][:, 2 * jp : 2 * jp + 2, :], in_=st["obank", b, jp][:])

            def store(b):
                nc.sync.dma_start(out=out_blocks[b], in_=st["y", b][:].rearrange("p j n -> p (j n)"))

            ops = {
                "X0": lambda b: s_widen(b, 0), "X1": lambda b: s_widen(b, 1), "X2": lambda b: s_widen(b, 2), "X3": lambda b: s_widen(b, 3),
                "T00": lambda b: h_turn(b, 0, 0), "T01": lambda b: h_turn(b, 0, 1), "T10": lambda b: h_turn(b, 1, 0), "T11": lambda b: h_turn(b, 1, 1),
                "E00": lambda b: v_scale(b, 0, 0), "E01": lambda b: v_scale(b, 0, 1), "E10": lambda b: v_scale(b, 1, 0), "E11": lambda b: v_scale(b, 1, 1),
                "QH": v_quant_h, "QZ": v_quant_z, "ST": store,
                "Te0": lambda b: eps_turn(b, 0), "Te1": lambda b: eps_turn(b, 1),
                "A0": lambda b: v_noise(b, 0), "A2": lambda b: v_noise(b, 1),
                "I0": lambda b: z_sum(b, 0), "I1": lambda b: z_sum(b, 1),
                "Mo0": lambda b: mm_out(b, 0), "Mo1": lambda b: mm_out(b, 1), "Y0": lambda b: s_tanh(b, 0), "Y1": lambda b: s_tanh(b, 1),
                "To0": lambda b: out_turn(b, 0), "To1": lambda b: out_turn(b, 1), "Z0": lambda b: out_copy(b, 0), "Z1": lambda b: out_copy(b, 1),
                "Ml0": lambda b: mm_ls(b, 0), "Ml1": lambda b: mm_ls(b, 1), "Ml2": lambda b: mm_ls(b, 2), "Ml3": lambda b: mm_ls(b, 3),
                "Mm0": lambda b: mm_mu(b, 0), "Mm1": lambda b: mm_mu(b, 1), "Mm2": lambda b: mm_mu(b, 2), "Mm3": lambda b: mm_mu(b, 3),
                "X_0": lambda b: s_exp(b, 0), "X_1": lambda b: s_exp(b, 1), "X_2": lambda b: s_exp(b, 2), "X_3": lambda b: s_exp(b, 3),
                "D0": lambda b: s_mu(b, 0), "D1": lambda b: s_mu(b, 1), "D2": lambda b: s_mu(b, 2), "D3": lambda b: s_mu(b, 3),
            }
            order = [
                ("I0", 3), ("T11", -1), ("QZ", 4), ("Mm3", 1), ("Ml3", 1), ("QH", 0),
                ("Ml2", 0), ("Z0", 7), ("D3", 1), ("Mm0", 1), ("E10", -1), ("A0", 1),
                ("X_3", 1), ("Te1", 1), ("T01", -1), ("X2", -3), ("X_2", 0), ("Mo1", 5),
                ("Ml0", 0), ("D0", 1), ("E11", -1), ("X1", -3), ("Mm1", 1), ("Y1", 5),
                ("X_0", 0), ("I1", 2), ("D1", 1), ("Mo0", 5), ("Y0", 5), ("A2", 1),
                ("E01", -1), ("To1", 6), ("X0", -3), ("T00", -1), ("Z1", 6), ("Ml1", 0),
                ("Mm2", 1), ("E00", -1), ("X3", -4), ("To0", 6), ("Te0", 0), ("T10", -2),
                ("X_1", 0), ("D2", 1), ("ST", 7),
            ]
            for s in range(min(lag for name, lag in order), NB + max(lag for name, lag in order)):
                for name, lag in order:
                    if 0 <= s - lag < NB:
                        ops[name](s - lag)
